import numpy as np
import ml_dtypes


def mxq(x, axis, fmt="e4m3"):
    dtype, down = {"e4m3": (ml_dtypes.float8_e4m3fn, 7), "e5m2": (ml_dtypes.float8_e5m2, 14)}[fmt]
    v = np.moveaxis(np.asarray(x, np.float32).astype(ml_dtypes.bfloat16).astype(np.float64), axis, -1)
    blocks = v.reshape(v.shape[:-1] + (-1, 32))
    amax = np.abs(blocks).max(-1, keepdims=True)
    byte = np.maximum(np.where(amax > 0, np.frexp(amax)[1] - 1 + 127, 0) - down, 1)
    scale = np.exp2(byte - 127.0)
    codes = (blocks / scale).astype(np.float32).astype(dtype).astype(np.float64)
    return np.moveaxis((codes * scale).reshape(v.shape), -1, axis)


WIDE = False


def mx_kscale(k):
    if not WIDE:
        return np.ones(k)
    levels = np.array([10, -10, 5, -5, 0])
    a = np.random.permutation(np.resize(levels, k // 512 * 4)).reshape(k // 512, 4)
    idx = np.arange(k)
    return np.exp2(a[idx // 512, idx % 128 // 32])


BF16 = ml_dtypes.bfloat16


def bf(x):
    return np.asarray(x, np.float32).astype(BF16)


def f64(x):
    return np.asarray(x).astype(np.float64)


B, W, MID = 4096, 256, 1024


def setup_inputs():
    s, t = mx_kscale(MID), mx_kscale(MID)
    return {"h3": bf(np.maximum(np.random.standard_normal((B, MID)), 0.0) * np.sqrt(2.0) * s),
            "w4": bf(np.random.standard_normal((MID, MID)) * np.sqrt(2.0 / MID) / s[:, None] * t),
            "b4": bf(np.random.standard_normal(MID) * 0.1 * t),
            "w5": bf(np.random.standard_normal((MID, W)) * 0.7 / np.sqrt(MID) / t[:, None]),
            "b5": bf(np.random.standard_normal(W) * 0.2),
            "x": bf(np.random.standard_normal((B, W))),
            "log_det_J": bf(np.random.standard_normal(B) * 0.1 * np.sqrt(W))}


def reference(h3, w4, b4, w5, b5, x, log_det_J):
    xf = f64(x)
    x1 = xf[:, 0::2]
    x2 = xf[:, 1::2]
    h4 = np.maximum((mxq(f64(h3), 1, "e4m3") @ mxq(f64(w4), 0, "e4m3")) + f64(b4), 0.0)
    bvec = (mxq(h4, 1, "e4m3") @ mxq(f64(w5), 0, "e4m3")) + f64(b5)
    b1t = np.tanh(bvec[:, 0::2])
    b2t = bvec[:, 1::2]
    y2 = x2 * np.exp(b1t) + b2t
    log_det = f64(log_det_J) + np.sum(b1t, axis=1)
    y = np.stack((x1, y2), axis=2).reshape(xf.shape)
    return (y, log_det)

@@ -1,0 +1,317 @@
+from contextlib import ExitStack
+
+import concourse.mybir as mybir
+from concourse.masks import make_identity
+
+BF16 = mybir.dt.bfloat16
+F32 = mybir.dt.float32
+U32 = mybir.dt.uint32
+U8 = mybir.dt.uint8
+FP8X4 = mybir.dt.float8_e4m3fn_x4
+ACT = mybir.ActivationFunctionType
+ALU = mybir.AluOpType
+
+P = 128
+PACK = 4
+K_PASS = P * PACK
+
+BATCH, MID, WIDTH = 4096, 1024, 256
+HALF = WIDTH // 2
+PASSES = MID // K_PASS
+MID_TILES = MID // P
+TILES = BATCH // P
+GROUP_TILES = 4
+GROUP = GROUP_TILES * P
+GROUPS = TILES // GROUP_TILES
+W4_PIECE = 512
+
+FLOPS = 2 * BATCH * MID * MID + 2 * BATCH * MID * WIDTH
+
+
+def tile_affinecoupling_pa_t_kernel(tc, h3, w4, b4, w5, b5, x, log_det_J, out_0, out_1):
+    nc = tc.nc
+    with ExitStack() as ctx:
+        keep = ctx.enter_context(tc.tile_pool(name="keep", bufs=1))
+        h3_pool = ctx.enter_context(tc.tile_pool(name="h3_pool", bufs=GROUPS))
+        stage = ctx.enter_context(tc.tile_pool(name="stage", bufs=2))
+        psum = ctx.enter_context(tc.psum_pool(name="psum", bufs=2))
+
+        h3_rows = h3.rearrange("(p t) k -> p t k", t=TILES)
+        x_rows = x.rearrange("(p t) c -> p t c", t=TILES)
+        y_rows = out_0.rearrange("(p t) c -> p t c", t=TILES)
+
+        w4_raw = keep.tile([P, PASSES, PACK, MID], BF16)
+        h3_raw = []
+        for n in range(GROUPS):
+            raw = h3_pool.tile([P, GROUP_TILES, MID], BF16, name="h3_raw")
+            h3_raw.append(raw)
+
+        def load_w4(piece):
+            cols = slice(piece * W4_PIECE, (piece + 1) * W4_PIECE)
+            for g in range(PASSES):
+                for u in range(2):
+                    first = K_PASS * g + 2 * P * u
+                    nc.sync.dma_start(
+                        out=w4_raw[:, g, 2 * u : 2 * u + 2, cols],
+                        in_=w4[first : first + 2 * P, cols].rearrange("(q e) c -> q e c", e=2),
+                    )
+
+        def load_h3(n):
+            nc.sync.dma_start(
+                out=h3_raw[n][:], in_=h3_rows[:, n * GROUP_TILES : (n + 1) * GROUP_TILES, :]
+            )
+
+        x_all = keep.tile([P, TILES, WIDTH], BF16)
+        load_w4(0)
+        load_h3(0)
+        load_w4(1)
+        load_h3(1)
+        nc.sync.dma_start(out=x_all[:], in_=x_rows)
+        for n in range(2, GROUPS):
+            load_h3(n)
+
+        b4_rows = keep.tile([P, P], BF16)
+        nc.vector.memset(b4_rows[:], 0.0)
+        nc.scalar.dma_start(out=b4_rows[0:MID_TILES, :], in_=b4.rearrange("(m p) -> m p", p=P))
+        w5_raw = keep.tile([P, PASSES, PACK, WIDTH], BF16)
+        nc.scalar.dma_start(
+            out=w5_raw[:].rearrange("p g j n -> p (g j) n"),
+            in_=w5.rearrange("(g j p) n -> p (g j) n", j=PACK, p=P),
+        )
+        b5_rows = keep.tile([P, WIDTH], BF16)
+        nc.scalar.dma_start(out=b5_rows[:], in_=b5.partition_broadcast(P))
+        ldj = keep.tile([P, TILES], BF16)
+        nc.scalar.dma_start(out=ldj[:], in_=log_det_J.rearrange("(p t) -> p t", t=TILES))
+
+        ident_f32 = keep.tile([P, P], F32)
+        make_identity(nc, ident_f32[:])
+        ident_bf16 = keep.tile([P, P], BF16)
+        make_identity(nc, ident_bf16[:])
+
+        b4_t = psum.tile([P, P], BF16, tag="xt")
+        nc.tensor.transpose(b4_t[:], b4_rows[:], ident_bf16[:])
+        b4_cols = keep.tile([P, MID_TILES], F32)
+        nc.vector.tensor_copy(out=b4_cols[:], in_=b4_t[:, 0:MID_TILES])
+
+        w4_codes = keep.tile([P, PASSES, MID], U32, align_bytes=64)
+        w4_scales = keep.tile([P, PASSES, MID], U8, align_bytes=64)
+
+        def pack_w4(piece):
+            cols = slice(piece * W4_PIECE, (piece + 1) * W4_PIECE)
+            grouped = []
+            for g in range(PASSES):
+                w4_grouped = stage.tile([P, W4_PIECE, PACK], BF16, align_bytes=64)
+                nc.vector.tensor_copy(
+                    out=w4_grouped[:].rearrange("p (c i) t -> p c t i", i=4),
+                    in_=w4_raw[:, g, :, cols].rearrange("p t (c i) -> p c t i", i=4),
+                )
+                grouped.append(w4_grouped)
+            for g in range(PASSES):
+                nc.vector.quantize_mx(
+                    out=w4_codes[:, g, cols].bitcast(FP8X4),
+                    scales=w4_scales[:, g, cols],
+                    in_=grouped[g][:].rearrange("p c t -> p (c t)"),
+                )
+
+        w5_codes = keep.tile([P, PASSES, WIDTH], U32, align_bytes=64)
+        w5_scales = keep.tile([P, PASSES, WIDTH], U8, align_bytes=64)
+        b5_planes = keep.tile([P, 2, HALF], F32)
+
+        def pack_w5():
+            w5_grouped = keep.tile([P, PASSES, WIDTH, PACK], BF16, align_bytes=64)
+            for g in range(PASSES):
+                nc.vector.tensor_copy(
+                    out=w5_grouped[:, g].rearrange("p (e c) j -> p e c j", e=2),
+                    in_=w5_raw[:, g].rearrange("p j (c e) -> p e c j", e=2),
+                )
+            nc.vector.tensor_copy(out=b5_planes[:], in_=b5_rows[:].rearrange("p (c e) -> p e c", e=2))
+            nc.vector.quantize_mx(
+                out=w5_codes[:].rearrange("p g n -> p (g n)").bitcast(FP8X4),
+                scales=w5_scales[:].rearrange("p g n -> p (g n)"),
+                in_=w5_grouped[:].rearrange("p g n j -> p (g n j)"),
+            )
+
+        live = {}
+        sums = keep.tile([P, TILES], F32)
+
+        def transpose_h3(n):
+            raw_words = h3_raw[n][:].bitcast(F32)
+            h3_grouped = stage.tile([P, PASSES, GROUP, PACK], BF16, align_bytes=64)
+            grouped_words = h3_grouped[:].bitcast(F32)
+            for t in range(GROUP_TILES):
+                xt = psum.tile([P, PASSES * 2, P], F32, tag="xt")
+                for block in range(PASSES * 2):
+                    nc.tensor.transpose(
+                        xt[:, block, :], raw_words[:, t, block * P : (block + 1) * P], ident_f32[:]
+                    )
+                nc.scalar.copy(
+                    out=grouped_words[:, :, t * P : (t + 1) * P, :],
+                    in_=xt[:].rearrange("p (g u) r -> p g r u", u=2),
+                )
+            live["h3_grouped", n] = h3_grouped
+
+        def quantise_h3(n):
+            h3_codes = stage.tile([P, PASSES, GROUP], U32, align_bytes=64)
+            h3_scales = stage.tile([P, PASSES, GROUP], U8, align_bytes=64)
+            for g in range(PASSES):
+                nc.vector.quantize_mx(
+                    out=h3_codes[:, g, :].bitcast(FP8X4),
+                    scales=h3_scales[:, g, :],
+                    in_=live["h3_grouped", n][:, g].rearrange("p b t -> p (b t)"),
+                )
+            live["h3_codes", n] = h3_codes
+            live["h3_scales", n] = h3_scales
+
+        def first_matmul(n, g2):
+            if g2 == 0:
+                h4_planes = stage.tile([P, MID_TILES, GROUP], BF16)
+                live["h4_planes", n] = h4_planes
+            for m in range(g2 * PACK, (g2 + 1) * PACK):
+                acc = psum.tile([P, GROUP], F32, tag="acc", bufs=4)
+                for g in range(PASSES):
+                    nc.tensor.matmul_mx(
+                        out=acc[:],
+                        lhsT=w4_codes[:, g, m * P : (m + 1) * P].bitcast(FP8X4),
+                        lhsT_scale=w4_scales[:, g, m * P : (m + 1) * P],
+                        rhs=live["h3_codes", n][:, g, :].bitcast(FP8X4),
+                        rhs_scale=live["h3_scales", n][:, g, :],
+                        start=(g == 0),
+                        stop=(g == PASSES - 1),
+                    )
+                nc.scalar.activation(
+                    out=live["h4_planes", n][:, m, :],
+                    in_=acc[:],
+                    func=ACT.Relu,
+                    bias=b4_cols[:, m : m + 1],
+                    scale=1.0,
+                )
+
+        def regroup_h4(n, g2):
+            h4_grouped = stage.tile([P, GROUP, PACK], BF16, align_bytes=64)
+            nc.vector.tensor_copy(
+                out=h4_grouped[:].rearrange("p (c i) j -> p c j i", i=4),
+                in_=live["h4_planes", n][:, g2 * PACK : (g2 + 1) * PACK, :].rearrange(
+                    "p j (c i) -> p c j i", i=4
+                ),
+            )
+            live["h4_grouped", n, g2] = h4_grouped
+
+        def quantise_h4(n, g2):
+            if g2 == 0:
+                h4_codes = stage.tile([P, PASSES, GROUP], U32, align_bytes=64)
+                h4_scales = stage.tile([P, PASSES, GROUP], U8, align_bytes=64)
+                live["h4_codes", n] = h4_codes
+                live["h4_scales", n] = h4_scales
+            nc.vector.quantize_mx(
+                out=live["h4_codes", n][:, g2, :].bitcast(FP8X4),
+                scales=live["h4_scales", n][:, g2, :],
+                in_=live["h4_grouped", n, g2][:].rearrange("p b j -> p (b j)"),
+            )
+
+        def second_matmul(n):
+            planes = stage.tile([P, GROUP_TILES, 2, HALF], F32)
+            for pair in range(GROUP_TILES // 2):
+                v = psum.tile([P, 2, WIDTH], F32, tag="v")
+                for i in range(2):
+                    rows = slice((2 * pair + i) * P, (2 * pair + i + 1) * P)
+                    for g in range(PASSES):
+                        nc.tensor.matmul_mx(
+                            out=v[:, i, :],
+                            lhsT=live["h4_codes", n][:, g, rows].bitcast(FP8X4),
+                            lhsT_scale=live["h4_scales", n][:, g, rows],
+                            rhs=w5_codes[:, g, :].bitcast(FP8X4),
+                            rhs_scale=w5_scales[:, g, :],
+                            start=(g == 0),
+                            stop=(g == PASSES - 1),
+                        )
+                live["v", n, pair] = v
+            live["planes", n] = planes
+
+        def add_b5(n):
+            for pair in range(GROUP_TILES // 2):
+                nc.vector.tensor_tensor(
+                    out=live["planes", n][:, 2 * pair : 2 * pair + 2].rearrange("p t e c -> p t (e c)"),
+                    in0=live["v", n, pair][:],
+                    in1=b5_planes[:].rearrange("p e c -> p (e c)").unsqueeze(1).to_broadcast([P, 2, WIDTH]),
+                    op=ALU.add,
+                )
+
+        def log_scale(n):
+            ls = stage.tile([P, GROUP_TILES, HALF], F32)
+            for t in range(GROUP_TILES):
+                tile_index = n * GROUP_TILES + t
+                nc.scalar.activation(
+                    out=ls[:, t, :],
+                    in_=live["planes", n][:, t, 0, :],
+                    func=ACT.Tanh,
+                    accum_out=sums[:, tile_index : tile_index + 1],
+                )
+            scale = stage.tile([P, GROUP_TILES, HALF], F32)
+            nc.scalar.activation(out=scale[:], in_=ls[:], func=ACT.Exp)
+            live["scale", n] = scale
+
+        def x_pairs(n):
+            return x_all[:, n * GROUP_TILES : (n + 1) * GROUP_TILES, :].rearrange("p t (c e) -> p t c e", e=2)
+
+        def scale_x(n):
+            scaled = stage.tile([P, GROUP_TILES, HALF], F32)
+            nc.vector.tensor_tensor(
+                out=scaled[:], in0=x_pairs(n)[:, :, :, 1], in1=live["scale", n][:], op=ALU.mult
+            )
+            live["scaled", n] = scaled
+
+        def shift_x(n):
+            planes = live["planes", n]
+            nc.vector.tensor_copy(out=planes[:, :, 0, :], in_=x_pairs(n)[:, :, :, 0])
+            nc.vector.tensor_tensor(
+                out=planes[:, :, 1, :], in0=planes[:, :, 1, :], in1=live["scaled", n][:], op=ALU.add
+            )
+
+        def store_y(n):
+            y = stage.tile([P, GROUP_TILES, HALF, 2], F32)
+            nc.vector.tensor_copy(out=y[:], in_=live["planes", n][:].rearrange("p t e c -> p t c e"))
+            nc.sync.dma_start(
+                out=y_rows[:, n * GROUP_TILES : (n + 1) * GROUP_TILES, :],
+                in_=y[:].rearrange("p t c e -> p t (c e)"),
+            )
+
+        pack_w4(0)
+        transpose_h3(0)
+        quantise_h3(0)
+        pack_w4(1)
+        pack_w5()
+        for n in range(GROUPS + 1):
+            ahead = n + 1 < GROUPS
+            now = n < GROUPS
+            behind = n >= 1
+            if ahead:
+                transpose_h3(n + 1)
+            if behind:
+                second_matmul(n - 1)
+            if ahead:
+                quantise_h3(n + 1)
+            if behind:
+                add_b5(n - 1)
+            if now:
+                first_matmul(n, 0)
+            if behind:
+                log_scale(n - 1)
+            if now:
+                regroup_h4(n, 0)
+            if behind:
+                scale_x(n - 1)
+            if now:
+                quantise_h4(n, 0)
+                first_matmul(n, 1)
+            if behind:
+                shift_x(n - 1)
+            if now:
+                regroup_h4(n, 1)
+            if behind:
+                store_y(n - 1)
+            if now:
+                quantise_h4(n, 1)
+
+        log_det = keep.tile([P, TILES], F32)
+        nc.vector.tensor_tensor(out=log_det[:], in0=sums[:], in1=ldj[:], op=ALU.add)
+        nc.sync.dma_start(out=out_1.rearrange("(p t) -> p t", t=TILES), in_=log_det[:])

@@ -24,6 +24,7 @@ GROUP_TILES = 4
 GROUP = GROUP_TILES * P
 GROUPS = TILES // GROUP_TILES
 W4_PIECE = 512
+XT_BANKS, ACC_BANKS, V_BANKS = 3, 3, 2
 
 FLOPS = 2 * BATCH * MID * MID + 2 * BATCH * MID * WIDTH
 
@@ -40,7 +41,10 @@ def tile_affinecoupling_pa_t_kernel(tc, h3, w4, b4, w5, b5, x, log_det_J, out_0,
         x_rows = x.rearrange("(p t) c -> p t c", t=TILES)
         y_rows = out_0.rearrange("(p t) c -> p t c", t=TILES)
 
-        w4_raw = keep.tile([P, PASSES, PACK, MID], BF16)
+        w4_raw = []
+        for piece in range(MID // W4_PIECE):
+            w4_piece = keep.tile([P, PASSES, PACK, W4_PIECE], BF16, name="w4_raw", bufs=MID // W4_PIECE)
+            w4_raw.append(w4_piece)
         h3_raw = []
         for n in range(GROUPS):
             raw = h3_pool.tile([P, GROUP_TILES, MID], BF16, name="h3_raw")
@@ -52,27 +56,27 @@ def tile_affinecoupling_pa_t_kernel(tc, h3, w4, b4, w5, b5, x, log_det_J, out_0,
                 for u in range(2):
                     first = K_PASS * g + 2 * P * u
                     nc.sync.dma_start(
-                        out=w4_raw[:, g, 2 * u : 2 * u + 2, cols],
+                        out=w4_raw[piece][:, g, 2 * u : 2 * u + 2, :],
                         in_=w4[first : first + 2 * P, cols].rearrange("(q e) c -> q e c", e=2),
                     )
 
         def load_h3(n):
-            nc.sync.dma_start(
-                out=h3_raw[n][:], in_=h3_rows[:, n * GROUP_TILES : (n + 1) * GROUP_TILES, :]
-            )
+            for t in range(GROUP_TILES):
+                nc.sync.dma_start(out=h3_raw[n][:, t, :], in_=h3_rows[:, n * GROUP_TILES + t, :])
 
+        b4_rows = keep.tile([P, P], BF16)
+        nc.vector.memset(b4_rows[:], 0.0)
+        nc.sync.dma_start(out=b4_rows[0:MID_TILES, :], in_=b4.rearrange("(m p) -> m p", p=P))
         x_all = keep.tile([P, TILES, WIDTH], BF16)
         load_w4(0)
         load_h3(0)
         load_w4(1)
         load_h3(1)
+        load_h3(2)
         nc.sync.dma_start(out=x_all[:], in_=x_rows)
-        for n in range(2, GROUPS):
+        for n in range(3, GROUPS):
             load_h3(n)
 
-        b4_rows = keep.tile([P, P], BF16)
-        nc.vector.memset(b4_rows[:], 0.0)
-        nc.scalar.dma_start(out=b4_rows[0:MID_TILES, :], in_=b4.rearrange("(m p) -> m p", p=P))
         w5_raw = keep.tile([P, PASSES, PACK, WIDTH], BF16)
         nc.scalar.dma_start(
             out=w5_raw[:].rearrange("p g j n -> p (g j) n"),
@@ -83,12 +87,16 @@ def tile_affinecoupling_pa_t_kernel(tc, h3, w4, b4, w5, b5, x, log_det_J, out_0,
         ldj = keep.tile([P, TILES], BF16)
         nc.scalar.dma_start(out=ldj[:], in_=log_det_J.rearrange("(p t) -> p t", t=TILES))
 
+        warm = keep.tile([P, 1], F32)
+        nc.vector.memset(warm[:], 0.0)
+        nc.scalar.activation(out=warm[:], in_=warm[:], func=ACT.Tanh)
+
         ident_f32 = keep.tile([P, P], F32)
         make_identity(nc, ident_f32[:])
         ident_bf16 = keep.tile([P, P], BF16)
         make_identity(nc, ident_bf16[:])
 
-        b4_t = psum.tile([P, P], BF16, tag="xt")
+        b4_t = psum.tile([P, P], BF16, tag="xt", bufs=XT_BANKS)
         nc.tensor.transpose(b4_t[:], b4_rows[:], ident_bf16[:])
         b4_cols = keep.tile([P, MID_TILES], F32)
         nc.vector.tensor_copy(out=b4_cols[:], in_=b4_t[:, 0:MID_TILES])
@@ -103,7 +111,7 @@ def tile_affinecoupling_pa_t_kernel(tc, h3, w4, b4, w5, b5, x, log_det_J, out_0,
                 w4_grouped = stage.tile([P, W4_PIECE, PACK], BF16, align_bytes=64)
                 nc.vector.tensor_copy(
                     out=w4_grouped[:].rearrange("p (c i) t -> p c t i", i=4),
-                    in_=w4_raw[:, g, :, cols].rearrange("p t (c i) -> p c t i", i=4),
+                    in_=w4_raw[piece][:, g].rearrange("p t (c i) -> p c t i", i=4),
                 )
                 grouped.append(w4_grouped)
             for g in range(PASSES):
@@ -139,7 +147,7 @@ def tile_affinecoupling_pa_t_kernel(tc, h3, w4, b4, w5, b5, x, log_det_J, out_0,
             h3_grouped = stage.tile([P, PASSES, GROUP, PACK], BF16, align_bytes=64)
             grouped_words = h3_grouped[:].bitcast(F32)
             for t in range(GROUP_TILES):
-                xt = psum.tile([P, PASSES * 2, P], F32, tag="xt")
+                xt = psum.tile([P, PASSES * 2, P], F32, tag="xt", bufs=XT_BANKS)
                 for block in range(PASSES * 2):
                     nc.tensor.transpose(
                         xt[:, block, :], raw_words[:, t, block * P : (block + 1) * P], ident_f32[:]
@@ -167,7 +175,7 @@ def tile_affinecoupling_pa_t_kernel(tc, h3, w4, b4, w5, b5, x, log_det_J, out_0,
                 h4_planes = stage.tile([P, MID_TILES, GROUP], BF16)
                 live["h4_planes", n] = h4_planes
             for m in range(g2 * PACK, (g2 + 1) * PACK):
-                acc = psum.tile([P, GROUP], F32, tag="acc", bufs=4)
+                acc = psum.tile([P, GROUP], F32, tag="acc", bufs=ACC_BANKS)
                 for g in range(PASSES):
                     nc.tensor.matmul_mx(
                         out=acc[:],
@@ -211,7 +219,7 @@ def tile_affinecoupling_pa_t_kernel(tc, h3, w4, b4, w5, b5, x, log_det_J, out_0,
         def second_matmul(n):
             planes = stage.tile([P, GROUP_TILES, 2, HALF], F32)
             for pair in range(GROUP_TILES // 2):
-                v = psum.tile([P, 2, WIDTH], F32, tag="v")
+                v = psum.tile([P, 2, WIDTH], F32, tag="v", bufs=V_BANKS)
                 for i in range(2):
                     rows = slice((2 * pair + i) * P, (2 * pair + i + 1) * P)
                     for g in range(PASSES):
@@ -254,6 +262,7 @@ def tile_affinecoupling_pa_t_kernel(tc, h3, w4, b4, w5, b5, x, log_det_J, out_0,
             return x_all[:, n * GROUP_TILES : (n + 1) * GROUP_TILES, :].rearrange("p t (c e) -> p t c e", e=2)
 
         def scale_x(n):
+            nc.vector.tensor_copy(out=live["planes", n][:, :, 0, :], in_=x_pairs(n)[:, :, :, 0])
             scaled = stage.tile([P, GROUP_TILES, HALF], F32)
             nc.vector.tensor_tensor(
                 out=scaled[:], in0=x_pairs(n)[:, :, :, 1], in1=live["scale", n][:], op=ALU.mult
@@ -262,7 +271,6 @@ def tile_affinecoupling_pa_t_kernel(tc, h3, w4, b4, w5, b5, x, log_det_J, out_0,
 
         def shift_x(n):
             planes = live["planes", n]
-            nc.vector.tensor_copy(out=planes[:, :, 0, :], in_=x_pairs(n)[:, :, :, 0])
             nc.vector.tensor_tensor(
                 out=planes[:, :, 1, :], in0=planes[:, :, 1, :], in1=live["scaled", n][:], op=ALU.add
             )
@@ -275,42 +283,45 @@ def tile_affinecoupling_pa_t_kernel(tc, h3, w4, b4, w5, b5, x, log_det_J, out_0,
                 in_=y[:].rearrange("p t c e -> p t (c e)"),
             )
 
-        pack_w4(0)
-        transpose_h3(0)
-        quantise_h3(0)
-        pack_w4(1)
-        pack_w5()
-        for n in range(GROUPS + 1):
-            ahead = n + 1 < GROUPS
-            now = n < GROUPS
-            behind = n >= 1
-            if ahead:
-                transpose_h3(n + 1)
-            if behind:
-                second_matmul(n - 1)
-            if ahead:
-                quantise_h3(n + 1)
-            if behind:
-                add_b5(n - 1)
-            if now:
+        def on(k):
+            return 0 <= k < GROUPS
+
+        def one_round(n):
+            if on(n - 1):
+                regroup_h4(n - 1, 1)
+            if on(n - 3):
+                shift_x(n - 3)
+            if on(n - 1):
+                quantise_h4(n - 1, 1)
+            if on(n - 3):
+                store_y(n - 3)
+            if on(n):
                 first_matmul(n, 0)
-            if behind:
-                log_scale(n - 1)
-            if now:
                 regroup_h4(n, 0)
-            if behind:
-                scale_x(n - 1)
-            if now:
+            if on(n + 1):
+                transpose_h3(n + 1)
+                quantise_h3(n + 1)
+            if on(n):
                 quantise_h4(n, 0)
+            if on(n - 1):
+                second_matmul(n - 1)
+                add_b5(n - 1)
+            if on(n - 2):
+                log_scale(n - 2)
+            if on(n):
                 first_matmul(n, 1)
-            if behind:
-                shift_x(n - 1)
-            if now:
-                regroup_h4(n, 1)
-            if behind:
-                store_y(n - 1)
-            if now:
-                quantise_h4(n, 1)
+            if on(n - 2):
+                scale_x(n - 2)
+
+        with tc.manual_schedule():
+            pack_w4(0)
+            transpose_h3(0)
+            quantise_h3(0)
+            pack_w4(1)
+            one_round(0)
+            pack_w5()
+            for n in range(1, GROUPS + 3):
+                one_round(n)
 
         log_det = keep.tile([P, TILES], F32)
         nc.vector.tensor_tensor(out=log_det[:], in0=sums[:], in1=ldj[:], op=ALU.add)

@@ -313,15 +313,14 @@ def tile_affinecoupling_pa_t_kernel(tc, h3, w4, b4, w5, b5, x, log_det_J, out_0,
             if on(n - 2):
                 scale_x(n - 2)
 
-        with tc.manual_schedule():
-            pack_w4(0)
-            transpose_h3(0)
-            quantise_h3(0)
-            pack_w4(1)
-            one_round(0)
-            pack_w5()
-            for n in range(1, GROUPS + 3):
-                one_round(n)
+        pack_w4(0)
+        transpose_h3(0)
+        quantise_h3(0)
+        pack_w4(1)
+        one_round(0)
+        pack_w5()
+        for n in range(1, GROUPS + 3):
+            one_round(n)
 
         log_det = keep.tile([P, TILES], F32)
         nc.vector.tensor_tensor(out=log_det[:], in0=sums[:], in1=ldj[:], op=ALU.add)

from contextlib import ExitStack

import concourse.mybir as mybir
from concourse.masks import make_identity

BF16 = mybir.dt.bfloat16
F32 = mybir.dt.float32
U32 = mybir.dt.uint32
U8 = mybir.dt.uint8
FP8X4 = mybir.dt.float8_e4m3fn_x4
ACT = mybir.ActivationFunctionType
ALU = mybir.AluOpType

P = 128
PACK = 4
K_PASS = P * PACK

BATCH, MID, WIDTH = 4096, 1024, 256
HALF = WIDTH // 2
PASSES = MID // K_PASS
MID_TILES = MID // P
TILES = BATCH // P
GROUP_TILES = 4
GROUP = GROUP_TILES * P
GROUPS = TILES // GROUP_TILES
W4_PIECE = 512
XT_BANKS, ACC_BANKS, V_BANKS = 3, 3, 2

FLOPS = 2 * BATCH * MID * MID + 2 * BATCH * MID * WIDTH


def tile_affinecoupling_pa_t_kernel(tc, h3, w4, b4, w5, b5, x, log_det_J, out_0, out_1):
    nc = tc.nc
    with ExitStack() as ctx:
        keep = ctx.enter_context(tc.tile_pool(name="keep", bufs=1))
        h3_pool = ctx.enter_context(tc.tile_pool(name="h3_pool", bufs=GROUPS))
        stage = ctx.enter_context(tc.tile_pool(name="stage", bufs=2))
        psum = ctx.enter_context(tc.psum_pool(name="psum", bufs=2))

        h3_rows = h3.rearrange("(p t) k -> p t k", t=TILES)
        x_rows = x.rearrange("(p t) c -> p t c", t=TILES)
        y_rows = out_0.rearrange("(p t) c -> p t c", t=TILES)

        w4_raw = []
        for piece in range(MID // W4_PIECE):
            w4_piece = keep.tile([P, PASSES, PACK, W4_PIECE], BF16, name="w4_raw", bufs=MID // W4_PIECE)
            w4_raw.append(w4_piece)
        h3_raw = []
        for n in range(GROUPS):
            raw = h3_pool.tile([P, GROUP_TILES, MID], BF16, name="h3_raw")
            h3_raw.append(raw)

        def load_w4(piece):
            cols = slice(piece * W4_PIECE, (piece + 1) * W4_PIECE)
            for g in range(PASSES):
                for u in range(2):
                    first = K_PASS * g + 2 * P * u
                    nc.sync.dma_start(
                        out=w4_raw[piece][:, g, 2 * u : 2 * u + 2, :],
                        in_=w4[first : first + 2 * P, cols].rearrange("(q e) c -> q e c", e=2),
                    )

        def load_h3(n):
            for t in range(GROUP_TILES):
                nc.sync.dma_start(out=h3_raw[n][:, t, :], in_=h3_rows[:, n * GROUP_TILES + t, :])

        b4_rows = keep.tile([P, P], BF16)
        nc.vector.memset(b4_rows[:], 0.0)
        nc.sync.dma_start(out=b4_rows[0:MID_TILES, :], in_=b4.rearrange("(m p) -> m p", p=P))
        x_all = keep.tile([P, TILES, WIDTH], BF16)
        load_w4(0)
        load_h3(0)
        load_w4(1)
        load_h3(1)
        load_h3(2)
        nc.sync.dma_start(out=x_all[:], in_=x_rows)
        for n in range(3, GROUPS):
            load_h3(n)

        w5_raw = keep.tile([P, PASSES, PACK, WIDTH], BF16)
        nc.scalar.dma_start(
            out=w5_raw[:].rearrange("p g j n -> p (g j) n"),
            in_=w5.rearrange("(g j p) n -> p (g j) n", j=PACK, p=P),
        )
        b5_rows = keep.tile([P, WIDTH], BF16)
        nc.scalar.dma_start(out=b5_rows[:], in_=b5.partition_broadcast(P))
        ldj = keep.tile([P, TILES], BF16)
        nc.scalar.dma_start(out=ldj[:], in_=log_det_J.rearrange("(p t) -> p t", t=TILES))

        warm = keep.tile([P, 1], F32)
        nc.vector.memset(warm[:], 0.0)
        nc.scalar.activation(out=warm[:], in_=warm[:], func=ACT.Tanh)

        ident_f32 = keep.tile([P, P], F32)
        make_identity(nc, ident_f32[:])
        ident_bf16 = keep.tile([P, P], BF16)
        make_identity(nc, ident_bf16[:])

        b4_t = psum.tile([P, P], BF16, tag="xt", bufs=XT_BANKS)
        nc.tensor.transpose(b4_t[:], b4_rows[:], ident_bf16[:])
        b4_cols = keep.tile([P, MID_TILES], F32)
        nc.vector.tensor_copy(out=b4_cols[:], in_=b4_t[:, 0:MID_TILES])

        w4_codes = keep.tile([P, PASSES, MID], U32, align_bytes=64)
        w4_scales = keep.tile([P, PASSES, MID], U8, align_bytes=64)

        def pack_w4(piece):
            cols = slice(piece * W4_PIECE, (piece + 1) * W4_PIECE)
            grouped = []
            for g in range(PASSES):
                w4_grouped = stage.tile([P, W4_PIECE, PACK], BF16, align_bytes=64)
                nc.vector.tensor_copy(
                    out=w4_grouped[:].rearrange("p (c i) t -> p c t i", i=4),
                    in_=w4_raw[piece][:, g].rearrange("p t (c i) -> p c t i", i=4),
                )
                grouped.append(w4_grouped)
            for g in range(PASSES):
                nc.vector.quantize_mx(
                    out=w4_codes[:, g, cols].bitcast(FP8X4),
                    scales=w4_scales[:, g, cols],
                    in_=grouped[g][:].rearrange("p c t -> p (c t)"),
                )

        w5_codes = keep.tile([P, PASSES, WIDTH], U32, align_bytes=64)
        w5_scales = keep.tile([P, PASSES, WIDTH], U8, align_bytes=64)
        b5_planes = keep.tile([P, 2, HALF], F32)

        def pack_w5():
            w5_grouped = keep.tile([P, PASSES, WIDTH, PACK], BF16, align_bytes=64)
            for g in range(PASSES):
                nc.vector.tensor_copy(
                    out=w5_grouped[:, g].rearrange("p (e c) j -> p e c j", e=2),
                    in_=w5_raw[:, g].rearrange("p j (c e) -> p e c j", e=2),
                )
            nc.vector.tensor_copy(out=b5_planes[:], in_=b5_rows[:].rearrange("p (c e) -> p e c", e=2))
            nc.vector.quantize_mx(
                out=w5_codes[:].rearrange("p g n -> p (g n)").bitcast(FP8X4),
                scales=w5_scales[:].rearrange("p g n -> p (g n)"),
                in_=w5_grouped[:].rearrange("p g n j -> p (g n j)"),
            )

        live = {}
        sums = keep.tile([P, TILES], F32)

        def transpose_h3(n):
            raw_words = h3_raw[n][:].bitcast(F32)
            h3_grouped = stage.tile([P, PASSES, GROUP, PACK], BF16, align_bytes=64)
            grouped_words = h3_grouped[:].bitcast(F32)
            for t in range(GROUP_TILES):
                xt = psum.tile([P, PASSES * 2, P], F32, tag="xt", bufs=XT_BANKS)
                for block in range(PASSES * 2):
                    nc.tensor.transpose(
                        xt[:, block, :], raw_words[:, t, block * P : (block + 1) * P], ident_f32[:]
                    )
                nc.scalar.copy(
                    out=grouped_words[:, :, t * P : (t + 1) * P, :],
                    in_=xt[:].rearrange("p (g u) r -> p g r u", u=2),
                )
            live["h3_grouped", n] = h3_grouped

        def quantise_h3(n):
            h3_codes = stage.tile([P, PASSES, GROUP], U32, align_bytes=64)
            h3_scales = stage.tile([P, PASSES, GROUP], U8, align_bytes=64)
            for g in range(PASSES):
                nc.vector.quantize_mx(
                    out=h3_codes[:, g, :].bitcast(FP8X4),
                    scales=h3_scales[:, g, :],
                    in_=live["h3_grouped", n][:, g].rearrange("p b t -> p (b t)"),
                )
            live["h3_codes", n] = h3_codes
            live["h3_scales", n] = h3_scales

        def first_matmul(n, g2):
            if g2 == 0:
                h4_planes = stage.tile([P, MID_TILES, GROUP], BF16)
                live["h4_planes", n] = h4_planes
            for m in range(g2 * PACK, (g2 + 1) * PACK):
                acc = psum.tile([P, GROUP], F32, tag="acc", bufs=ACC_BANKS)
                for g in range(PASSES):
                    nc.tensor.matmul_mx(
                        out=acc[:],
                        lhsT=w4_codes[:, g, m * P : (m + 1) * P].bitcast(FP8X4),
                        lhsT_scale=w4_scales[:, g, m * P : (m + 1) * P],
                        rhs=live["h3_codes", n][:, g, :].bitcast(FP8X4),
                        rhs_scale=live["h3_scales", n][:, g, :],
                        start=(g == 0),
                        stop=(g == PASSES - 1),
                    )
                nc.scalar.activation(
                    out=live["h4_planes", n][:, m, :],
                    in_=acc[:],
                    func=ACT.Relu,
                    bias=b4_cols[:, m : m + 1],
                    scale=1.0,
                )

        def regroup_h4(n, g2):
            h4_grouped = stage.tile([P, GROUP, PACK], BF16, align_bytes=64)
            nc.vector.tensor_copy(
                out=h4_grouped[:].rearrange("p (c i) j -> p c j i", i=4),
                in_=live["h4_planes", n][:, g2 * PACK : (g2 + 1) * PACK, :].rearrange(
                    "p j (c i) -> p c j i", i=4
                ),
            )
            live["h4_grouped", n, g2] = h4_grouped

        def quantise_h4(n, g2):
            if g2 == 0:
                h4_codes = stage.tile([P, PASSES, GROUP], U32, align_bytes=64)
                h4_scales = stage.tile([P, PASSES, GROUP], U8, align_bytes=64)
                live["h4_codes", n] = h4_codes
                live["h4_scales", n] = h4_scales
            nc.vector.quantize_mx(
                out=live["h4_codes", n][:, g2, :].bitcast(FP8X4),
                scales=live["h4_scales", n][:, g2, :],
                in_=live["h4_grouped", n, g2][:].rearrange("p b j -> p (b j)"),
            )

        def second_matmul(n):
            planes = stage.tile([P, GROUP_TILES, 2, HALF], F32)
            for pair in range(GROUP_TILES // 2):
                v = psum.tile([P, 2, WIDTH], F32, tag="v", bufs=V_BANKS)
                for i in range(2):
                    rows = slice((2 * pair + i) * P, (2 * pair + i + 1) * P)
                    for g in range(PASSES):
                        nc.tensor.matmul_mx(
                            out=v[:, i, :],
                            lhsT=live["h4_codes", n][:, g, rows].bitcast(FP8X4),
                            lhsT_scale=live["h4_scales", n][:, g, rows],
                            rhs=w5_codes[:, g, :].bitcast(FP8X4),
                            rhs_scale=w5_scales[:, g, :],
                            start=(g == 0),
                            stop=(g == PASSES - 1),
                        )
                live["v", n, pair] = v
            live["planes", n] = planes

        def add_b5(n):
            for pair in range(GROUP_TILES // 2):
                nc.vector.tensor_tensor(
                    out=live["planes", n][:, 2 * pair : 2 * pair + 2].rearrange("p t e c -> p t (e c)"),
                    in0=live["v", n, pair][:],
                    in1=b5_planes[:].rearrange("p e c -> p (e c)").unsqueeze(1).to_broadcast([P, 2, WIDTH]),
                    op=ALU.add,
                )

        def log_scale(n):
            ls = stage.tile([P, GROUP_TILES, HALF], F32)
            for t in range(GROUP_TILES):
                tile_index = n * GROUP_TILES + t
                nc.scalar.activation(
                    out=ls[:, t, :],
                    in_=live["planes", n][:, t, 0, :],
                    func=ACT.Tanh,
                    accum_out=sums[:, tile_index : tile_index + 1],
                )
            scale = stage.tile([P, GROUP_TILES, HALF], F32)
            nc.scalar.activation(out=scale[:], in_=ls[:], func=ACT.Exp)
            live["scale", n] = scale

        def x_pairs(n):
            return x_all[:, n * GROUP_TILES : (n + 1) * GROUP_TILES, :].rearrange("p t (c e) -> p t c e", e=2)

        def scale_x(n):
            nc.vector.tensor_copy(out=live["planes", n][:, :, 0, :], in_=x_pairs(n)[:, :, :, 0])
            scaled = stage.tile([P, GROUP_TILES, HALF], F32)
            nc.vector.tensor_tensor(
                out=scaled[:], in0=x_pairs(n)[:, :, :, 1], in1=live["scale", n][:], op=ALU.mult
            )
            live["scaled", n] = scaled

        def shift_x(n):
            planes = live["planes", n]
            nc.vector.tensor_tensor(
                out=planes[:, :, 1, :], in0=planes[:, :, 1, :], in1=live["scaled", n][:], op=ALU.add
            )

        def store_y(n):
            y = stage.tile([P, GROUP_TILES, HALF, 2], F32)
            nc.vector.tensor_copy(out=y[:], in_=live["planes", n][:].rearrange("p t e c -> p t c e"))
            nc.sync.dma_start(
                out=y_rows[:, n * GROUP_TILES : (n + 1) * GROUP_TILES, :],
                in_=y[:].rearrange("p t c e -> p t (c e)"),
            )

        def on(k):
            return 0 <= k < GROUPS

        def one_round(n):
            if on(n - 1):
                regroup_h4(n - 1, 1)
            if on(n - 3):
                shift_x(n - 3)
            if on(n - 1):
                quantise_h4(n - 1, 1)
            if on(n - 3):
                store_y(n - 3)
            if on(n):
                first_matmul(n, 0)
                regroup_h4(n, 0)
            if on(n + 1):
                transpose_h3(n + 1)
                quantise_h3(n + 1)
            if on(n):
                quantise_h4(n, 0)
            if on(n - 1):
                second_matmul(n - 1)
                add_b5(n - 1)
            if on(n - 2):
                log_scale(n - 2)
            if on(n):
                first_matmul(n, 1)
            if on(n - 2):
                scale_x(n - 2)

        pack_w4(0)
        transpose_h3(0)
        quantise_h3(0)
        pack_w4(1)
        one_round(0)
        pack_w5()
        for n in range(1, GROUPS + 3):
            one_round(n)

        log_det = keep.tile([P, TILES], F32)
        nc.vector.tensor_tensor(out=log_det[:], in0=sums[:], in1=ldj[:], op=ALU.add)
        nc.sync.dma_start(out=out_1.rearrange("(p t) -> p t", t=TILES), in_=log_det[:])
